import numpy as np
import ml_dtypes

BF16 = ml_dtypes.bfloat16


def bf(x):
    return np.asarray(x, np.float32).astype(BF16)


def f32(x):
    return np.asarray(x, np.float32)


def f64(x):
    return np.asarray(x).astype(np.float64)


def striped(idx):
    return np.tile(idx.reshape(-1, 16).T, (8, 1))


S, D, Q, M, N = 4096, 128, 256, 512, 1024


def setup_inputs():
    return {"table": bf(np.random.standard_normal((D, S))), "w": bf(np.random.standard_normal((D, M)) / np.sqrt(D)), "offs": striped(np.random.permutation(np.tile(np.arange(S), 2))[:N])}


def reference(table, w, offs):
    idx = offs[:16].T.reshape(-1)
    p = f64(w).T @ f64(table)[:, idx]
    p[:Q] = p[:Q] * (1.0 / np.sqrt(D))
    return p

@@ -1,0 +1,46 @@
+import math
+
+import concourse.mybir as mybir
+
+P = 128
+S = 4096
+M = 512
+N = 1024
+BANK = 512
+PSUM_BANKS = 8
+PIECE = 256
+BLOCKS = M // P
+PIECES = N // PIECE
+QUERY_BLOCKS = 256 // P
+QUERY_FACTOR = 1.0 / math.sqrt(128.0)
+
+FLOPS = 2 * P * M * N
+
+BF16, F32, U16 = mybir.dt.bfloat16, mybir.dt.float32, mybir.dt.uint16
+
+
+def tile_widthchartransformermlpheaderfastpos_kernel(tc, table, w, offs, out):
+    nc = tc.nc
+    with (
+        tc.tile_pool(name="held", bufs=1) as held,
+        tc.tile_pool(name="staging", bufs=BLOCKS * PIECES) as staging,
+        tc.psum_pool(name="psum", bufs=PSUM_BANKS) as psum,
+    ):
+        window = held.tile([P, S], BF16, name="window")
+        nc.sync.dma_start(window[:], table)
+        offsets = held.tile([P, N // 16], U16, name="offsets")
+        nc.sync.dma_start(offsets[:], offs)
+        weights = held.tile([P, M], BF16, name="weights")
+        nc.scalar.dma_start(weights[:, 0:P], w[:, 0:P])
+        nc.sync.dma_start(weights[:, P:M], w[:, P:M])
+
+        for block in range(BLOCKS):
+            factor = QUERY_FACTOR if block < QUERY_BLOCKS else 1.0
+            rows = slice(block * P, (block + 1) * P)
+            for piece in range(PIECES):
+                picked = window[:].indirect(offsets[:, piece * (PIECE // 16) : (piece + 1) * (PIECE // 16)])
+                product = psum.tile([P, BANK], F32, name="product")
+                nc.tensor.matmul(product[:, 0:PIECE], weights[:, rows], picked, start=True, stop=True)
+                scaled = staging.tile([P, PIECE], F32, name="scaled")
+                nc.vector.tensor_scalar_mul(scaled[:], product[:, 0:PIECE], factor)
+                nc.sync.dma_start(out[rows, piece * PIECE : (piece + 1) * PIECE], scaled[:])

@@ -27,9 +27,10 @@ def tile_widthchartransformermlpheaderfastpos_kernel(tc, table, w, offs, out):
         tc.psum_pool(name="psum", bufs=PSUM_BANKS) as psum,
     ):
         window = held.tile([P, S], BF16, name="window")
-        nc.sync.dma_start(window[:], table)
+        nc.sync.dma_start(window[:, 0 : S // 2], table[:, 0 : S // 2])
         offsets = held.tile([P, N // 16], U16, name="offsets")
         nc.sync.dma_start(offsets[:], offs)
+        nc.sync.dma_start(window[:, S // 2 : S], table[:, S // 2 : S])
         weights = held.tile([P, M], BF16, name="weights")
         nc.scalar.dma_start(weights[:, 0:P], w[:, 0:P])
         nc.sync.dma_start(weights[:, P:M], w[:, P:M])

@@ -36,12 +36,14 @@ def tile_widthchartransformermlpheaderfastpos_kernel(tc, table, w, offs, out):
         nc.sync.dma_start(weights[:, P:M], w[:, P:M])
 
         for block in range(BLOCKS):
-            factor = QUERY_FACTOR if block < QUERY_BLOCKS else 1.0
             rows = slice(block * P, (block + 1) * P)
             for piece in range(PIECES):
                 picked = window[:].indirect(offsets[:, piece * (PIECE // 16) : (piece + 1) * (PIECE // 16)])
                 product = psum.tile([P, BANK], F32, name="product")
                 nc.tensor.matmul(product[:, 0:PIECE], weights[:, rows], picked, start=True, stop=True)
                 scaled = staging.tile([P, PIECE], F32, name="scaled")
-                nc.vector.tensor_scalar_mul(scaled[:], product[:, 0:PIECE], factor)
+                if block < QUERY_BLOCKS:
+                    nc.vector.tensor_scalar_mul(scaled[:], product[:, 0:PIECE], QUERY_FACTOR)
+                else:
+                    nc.vector.tensor_copy(scaled[:], product[:, 0:PIECE])
                 nc.sync.dma_start(out[rows, piece * PIECE : (piece + 1) * PIECE], scaled[:])

import math

import concourse.mybir as mybir

P = 128
S = 4096
M = 512
N = 1024
BANK = 512
PSUM_BANKS = 8
PIECE = 256
BLOCKS = M // P
PIECES = N // PIECE
QUERY_BLOCKS = 256 // P
QUERY_FACTOR = 1.0 / math.sqrt(128.0)

FLOPS = 2 * P * M * N

BF16, F32, U16 = mybir.dt.bfloat16, mybir.dt.float32, mybir.dt.uint16


def tile_widthchartransformermlpheaderfastpos_kernel(tc, table, w, offs, out):
    nc = tc.nc
    with (
        tc.tile_pool(name="held", bufs=1) as held,
        tc.tile_pool(name="staging", bufs=BLOCKS * PIECES) as staging,
        tc.psum_pool(name="psum", bufs=PSUM_BANKS) as psum,
    ):
        window = held.tile([P, S], BF16, name="window")
        nc.sync.dma_start(window[:, 0 : S // 2], table[:, 0 : S // 2])
        offsets = held.tile([P, N // 16], U16, name="offsets")
        nc.sync.dma_start(offsets[:], offs)
        nc.sync.dma_start(window[:, S // 2 : S], table[:, S // 2 : S])
        weights = held.tile([P, M], BF16, name="weights")
        nc.scalar.dma_start(weights[:, 0:P], w[:, 0:P])
        nc.sync.dma_start(weights[:, P:M], w[:, P:M])

        for block in range(BLOCKS):
            rows = slice(block * P, (block + 1) * P)
            for piece in range(PIECES):
                picked = window[:].indirect(offsets[:, piece * (PIECE // 16) : (piece + 1) * (PIECE // 16)])
                product = psum.tile([P, BANK], F32, name="product")
                nc.tensor.matmul(product[:, 0:PIECE], weights[:, rows], picked, start=True, stop=True)
                scaled = staging.tile([P, PIECE], F32, name="scaled")
                if block < QUERY_BLOCKS:
                    nc.vector.tensor_scalar_mul(scaled[:], product[:, 0:PIECE], QUERY_FACTOR)
                else:
                    nc.vector.tensor_copy(scaled[:], product[:, 0:PIECE])
                nc.sync.dma_start(out[rows, piece * PIECE : (piece + 1) * PIECE], scaled[:])
